import numpy as np
import ml_dtypes


def mxq(x, axis, fmt="e4m3"):
    dtype, down = {"e4m3": (ml_dtypes.float8_e4m3fn, 7), "e5m2": (ml_dtypes.float8_e5m2, 14)}[fmt]
    v = np.moveaxis(np.asarray(x, np.float32).astype(ml_dtypes.bfloat16).astype(np.float64), axis, -1)
    blocks = v.reshape(v.shape[:-1] + (-1, 32))
    amax = np.abs(blocks).max(-1, keepdims=True)
    byte = np.maximum(np.where(amax > 0, np.frexp(amax)[1] - 1 + 127, 0) - down, 1)
    scale = np.exp2(byte - 127.0)
    codes = (blocks / scale).astype(np.float32).astype(dtype).astype(np.float64)
    return np.moveaxis((codes * scale).reshape(v.shape), -1, axis)


WIDE = False


def mx_kscale(k):
    if not WIDE:
        return np.ones(k)
    levels = np.array([10, -10, 5, -5, 0])
    if k % 512:
        return np.exp2(np.random.permutation(np.resize(levels, k // 32))).repeat(32)
    a = np.empty((k // 512, 16))
    for p in range(k // 512):
        a[p, :8] = np.random.permutation(np.resize(levels, 8))
        for g in range(8):
            far = levels[np.abs(levels - a[p, g]) >= 10]
            a[p, g + 8] = far[np.random.randint(len(far))]
    return np.exp2(a.ravel()).repeat(32)


BF16 = ml_dtypes.bfloat16


def bf(x):
    return np.asarray(x, np.float32).astype(BF16)


def f64(x):
    return np.asarray(x).astype(np.float64)


N, L, D, M = 512, 32, 512, 512


def l2norm(v):
    n = np.sqrt((v * v).sum(axis=-1, keepdims=True))
    return v / np.maximum(n, 1e-12)


def setup_inputs():
    s = mx_kscale(D)
    amp_f = 0.5 + 1.5 * np.random.random((N, L))[:, :, None]
    amp_v = 0.5 + 1.5 * np.random.random(N)[:, None]
    return {"feature": bf(np.random.standard_normal((N, L, D)) * amp_f * s),
            "aspect_v": bf(np.random.standard_normal((N, D)) * amp_v * s),
            "W": bf(np.random.standard_normal((M, D)) * np.sqrt(2.0 / (D + M)) / s),
            "b": bf(np.random.standard_normal(M) * 0.2)}


def reference(feature, aspect_v, W, b):
    wq = mxq(f64(W), 1, "e4m3")
    q = l2norm((mxq(f64(aspect_v), 1, "e4m3") @ wq.T) + f64(b))
    fn = l2norm((mxq(f64(feature), 2, "e4m3") @ wq.T) + f64(b))
    return q, fn.mean(axis=1)

@@ -1,0 +1,271 @@
+from contextlib import ExitStack
+
+import concourse.mybir as mybir
+from concourse.masks import make_identity
+
+F32 = mybir.dt.float32
+BF16 = mybir.dt.bfloat16
+U32 = mybir.dt.uint32
+U8 = mybir.dt.uint8
+FP8X4 = mybir.dt.float8_e4m3fn_x4
+ADD = mybir.AluOpType.add
+MULT = mybir.AluOpType.mult
+POW = mybir.AluOpType.pow
+SQUARE = mybir.ActivationFunctionType.Square
+
+P = 128
+D_IN = 512
+D_OUT = 512
+TOKENS = 32
+TILES = 4
+FOLDED = 2
+KEPT = TILES - FOLDED
+assert FOLDED <= KEPT
+BATCH_ROWS = TILES * P
+GROUP_BATCHES = 2
+GROUP_TILES = GROUP_BATCHES * TILES
+GROUP_ROWS = GROUP_TILES * P
+GROUP_SEGMENTS = GROUP_ROWS // TOKENS
+SEGMENT_PARTITIONS = TOKENS // GROUP_TILES
+BLOCK_GROUPS = P // GROUP_SEGMENTS
+BLOCK_BATCHES = BLOCK_GROUPS * GROUP_BATCHES
+OUT_SLICES = D_OUT // P
+BATCH_SLICES = OUT_SLICES // GROUP_BATCHES
+WORDS = D_IN // 2
+BANK_TILES = 2
+BANKS = TILES // BANK_TILES
+ROW_BUFFERS = 4
+SUM_LAG = 4
+TINY = 1e-24
+
+FLOPS = 2 * (512 * 32 + 512) * D_IN * D_OUT
+
+
+def tile_linearattention_pa_t_kernel(tc, feature, aspect_v, W, b, out_0, out_1):
+    nc = tc.nc
+    tokens = feature.flatten_outer_dims()
+    feature_batches = tokens.shape[0] // BATCH_ROWS
+    aspect_batch = feature_batches
+    batches = feature_batches + 1
+
+    with ExitStack() as ctx:
+        ctx.enter_context(tc.manual_schedule())
+        const = ctx.enter_context(tc.tile_pool(name="const", bufs=1))
+        rows_pool = ctx.enter_context(tc.tile_pool(name="rows", bufs=ROW_BUFFERS))
+        grouped_pool = ctx.enter_context(tc.tile_pool(name="grouped", bufs=2))
+        codes_pool = ctx.enter_context(tc.tile_pool(name="codes", bufs=2))
+        y_pool = ctx.enter_context(tc.tile_pool(name="y", bufs=(SUM_LAG + GROUP_BATCHES + 1) * TILES))
+        weights_pool = ctx.enter_context(tc.tile_pool(name="weights", bufs=SUM_LAG + GROUP_BATCHES + 1))
+        squares_pool = ctx.enter_context(tc.tile_pool(name="squares", bufs=TILES))
+        norm_pool = ctx.enter_context(tc.tile_pool(name="norm", bufs=3))
+        fm_pool = ctx.enter_context(tc.tile_pool(name="fm", bufs=2))
+        words_psum = ctx.enter_context(tc.psum_pool(name="words_psum", bufs=BANKS))
+        product_psum = ctx.enter_context(tc.psum_pool(name="product_psum", bufs=TILES))
+        fm_t_psum = ctx.enter_context(tc.psum_pool(name="fm_t_psum", bufs=1))
+        fm_psum = ctx.enter_context(tc.psum_pool(name="fm_psum", bufs=1))
+
+        rows_of = {}
+        banks_of = {}
+        grouped_of = {}
+        codes_of = {}
+        scales_of = {}
+        y_of = {}
+        sumsq_of = {}
+        floored_of = {}
+        inverse_of = {}
+        weights_of = {}
+        ratio_of = {}
+        fm_t_of = {}
+        fm_t_sbuf_of = {}
+
+        def load(n, dram_view):
+            rows = rows_pool.tile([P, TILES * D_IN], BF16, name="rows")
+            nc.sync.dma_start(out=rows[:].rearrange("p (j k) -> p j k", j=TILES), in_=dram_view)
+            rows_of[n] = rows
+
+        def load_batch(n):
+            if n == aspect_batch:
+                load(n, aspect_v.rearrange("(p j) k -> p j k", j=TILES))
+            else:
+                group, part = divmod(n, GROUP_BATCHES)
+                group_rows = tokens[group * GROUP_ROWS : (group + 1) * GROUP_ROWS, :]
+                by_partition = group_rows.rearrange("(p j) k -> p j k", j=GROUP_TILES)
+                load(n, by_partition[:, part * TILES : (part + 1) * TILES, :])
+
+        def transpose(n):
+            words = rows_of[n][:].bitcast(F32)
+            blocks = BANK_TILES * WORDS // P
+            banks_of[n] = []
+            for h in range(BANKS):
+                bank = words_psum.tile([P, BANK_TILES * WORDS], F32, name="bank")
+                for block in range(blocks):
+                    j, u = divmod(h * blocks + block, 2)
+                    nc.tensor.transpose(
+                        out=bank[:, block * P : (block + 1) * P],
+                        in_=words[:, j * WORDS + u : (j + 1) * WORDS : 2],
+                        identity=identity[:],
+                    )
+                banks_of[n].append(bank)
+
+        def regroup(n):
+            grouped = grouped_pool.tile([P, TILES * P * 4], BF16, name="grouped", align_bytes=64)
+            pairs = grouped[:].bitcast(F32).rearrange("p (h j r u) -> p h j r u", h=BANKS, j=BANK_TILES, u=2)
+            for h in range(BANKS):
+                nc.scalar.copy(
+                    out=pairs[:, h],
+                    in_=banks_of[n][h][:].rearrange("p (j u r) -> p j r u", j=BANK_TILES, u=2),
+                )
+            grouped_of[n] = grouped
+
+        def quantise(n, pool):
+            codes = pool.tile([P, TILES * P], U32, name="codes", align_bytes=64)
+            scales = pool.tile([P, TILES * P], U8, name="scales", align_bytes=64)
+            nc.vector.quantize_mx(out=codes[:].bitcast(FP8X4), scales=scales[:], in_=grouped_of[n][:])
+            codes_of[n] = codes
+            scales_of[n] = scales
+
+        def multiply(n, j):
+            if j == 0:
+                sumsq = norm_pool.tile([P, TILES], F32, name="sumsq")
+                sumsq_of[n] = sumsq
+            cols = slice(j * P, (j + 1) * P)
+            product = product_psum.tile([P, D_OUT], F32, name="product")
+            nc.tensor.matmul_mx(
+                out=product[:],
+                lhsT=codes_of[n][:, cols].bitcast(FP8X4),
+                lhsT_scale=scales_of[n][:, cols],
+                rhs=codes_of["W"][:].bitcast(FP8X4),
+                rhs_scale=scales_of["W"][:],
+                start=True,
+                stop=True,
+            )
+            y = y_pool.tile([P, D_OUT], F32, name="y")
+            y_of[n, j] = y
+            nc.vector.tensor_tensor(out=y[:], in0=product[:], in1=bias[:], op=ADD)
+            squares = squares_pool.tile([P, D_OUT], BF16, name="squares")
+            nc.scalar.activation(out=squares[:], in_=y[:], func=SQUARE, accum_out=sumsq_of[n][:, j : j + 1])
+
+        def norms(n):
+            floored = norm_pool.tile([P, TILES], F32, name="floored")
+            inverse = norm_pool.tile([P, TILES], F32, name="inverse")
+            nc.gpsimd.tensor_scalar_max(out=floored[:], in0=sumsq_of[n][:], scalar1=TINY)
+            nc.gpsimd.tensor_tensor(out=inverse[:], in0=floored[:], in1=minus_half[:], op=POW)
+            floored_of[n] = floored
+            inverse_of[n] = inverse
+
+        def token_weights(n):
+            inverse = inverse_of[n]
+            norm = norm_pool.tile([P, FOLDED], F32, name="norm")
+            ratio = norm_pool.tile([P, FOLDED], F32, name="ratio")
+            weights = weights_pool.tile([P, KEPT, GROUP_SEGMENTS], F32, name="weights")
+            nc.gpsimd.tensor_tensor(out=norm[:], in0=floored_of[n][:, :FOLDED], in1=inverse[:, :FOLDED], op=MULT)
+            nc.gpsimd.tensor_tensor(out=ratio[:], in0=norm[:], in1=inverse[:, KEPT:], op=MULT)
+            nc.gpsimd.tensor_tensor(
+                out=weights[:],
+                in0=membership[:].unsqueeze(1).to_broadcast([P, KEPT, GROUP_SEGMENTS]),
+                in1=inverse[:, :KEPT].unsqueeze(2).to_broadcast([P, KEPT, GROUP_SEGMENTS]),
+                op=MULT,
+            )
+            weights_of[n] = weights
+            ratio_of[n] = ratio
+
+        def fold(n, i):
+            kept = y_of[n, i]
+            nc.vector.scalar_tensor_tensor(
+                out=kept[:], in0=y_of[n, KEPT + i][:], scalar=ratio_of[n][:, i : i + 1], in1=kept[:], op0=MULT, op1=ADD
+            )
+
+        def reduce_tokens(group, s):
+            block, place = divmod(group, BLOCK_GROUPS)
+            if place == 0 and s == 0:
+                fm_t = fm_t_psum.tile([P, OUT_SLICES * P], F32, name="fm_t")
+                fm_t_of[block] = fm_t
+            first = s * P + place * GROUP_SEGMENTS
+            for tile in range(GROUP_BATCHES * KEPT):
+                part, j = divmod(tile, KEPT)
+                n = group * GROUP_BATCHES + part
+                nc.tensor.matmul(
+                    out=fm_t_of[block][:, first : first + GROUP_SEGMENTS],
+                    lhsT=y_of[n, j][:, s * P : (s + 1) * P],
+                    rhs=weights_of[n][:, j, :],
+                    start=(tile == 0),
+                    stop=(tile == GROUP_BATCHES * KEPT - 1),
+                )
+
+        def collect_block(block):
+            fm_t_sbuf = fm_pool.tile([P, OUT_SLICES * P], F32, name="fm_t_sbuf")
+            nc.vector.tensor_copy(out=fm_t_sbuf[:], in_=fm_t_of[block][:])
+            fm_t_sbuf_of[block] = fm_t_sbuf
+
+        def store_block(block):
+            fm_bank = fm_psum.tile([P, D_OUT], F32, name="fm_bank")
+            for s in range(OUT_SLICES):
+                cols = slice(s * P, (s + 1) * P)
+                nc.tensor.transpose(out=fm_bank[:, cols], in_=fm_t_sbuf_of[block][:, cols], identity=identity[:])
+            fm = fm_pool.tile([P, D_OUT], F32, name="fm")
+            nc.scalar.copy(out=fm[:], in_=fm_bank[:])
+            nc.sync.dma_start(out=out_1[block * P : (block + 1) * P, :], in_=fm[:])
+
+        def store_q(n):
+            inverse = inverse_of[n]
+            q_rows = out_0.rearrange("(p j) m -> p j m", j=TILES)
+            for j in range(TILES):
+                y = y_of[n, j]
+                nc.vector.tensor_scalar_mul(out=y[:], in0=y[:], scalar1=inverse[:, j : j + 1])
+                nc.sync.dma_start(out=q_rows[:, j, :], in_=y[:])
+
+        load("W", W.rearrange("(j p) k -> p j k", p=P))
+        for n in range(ROW_BUFFERS - 1):
+            load_batch(n)
+        bias = const.tile([P, D_OUT], BF16, name="bias")
+        nc.scalar.dma_start(out=bias[:], in_=b.partition_broadcast(P))
+        identity = const.tile([P, P], F32, name="identity")
+        make_identity(nc, identity[:])
+        minus_half = const.tile([P, TILES], F32, name="minus_half")
+        nc.vector.memset(minus_half[:], -0.5)
+        membership = const.tile([P, GROUP_SEGMENTS], F32, name="membership")
+        nc.vector.tensor_reduce(
+            out=membership[:],
+            in_=identity[:].rearrange("p (c i) -> p c i", i=SEGMENT_PARTITIONS),
+            axis=mybir.AxisListType.X,
+            op=ADD,
+        )
+        nc.vector.tensor_scalar_mul(out=membership[:], in0=membership[:], scalar1=1.0 / TOKENS)
+
+        transpose("W")
+        regroup("W")
+        quantise("W", const)
+
+        def in_range(n, end):
+            return 0 <= n < end
+
+        for t in range(-2, batches + SUM_LAG):
+            summed, stored = t - SUM_LAG, t - SUM_LAG - 1
+            if in_range(t + ROW_BUFFERS + 1, batches):
+                load_batch(t + ROW_BUFFERS + 1)
+            if in_range(stored, feature_batches) and stored % BLOCK_BATCHES == BLOCK_BATCHES - 1:
+                store_block(stored // BLOCK_BATCHES)
+            if in_range(t + 2, batches):
+                transpose(t + 2)
+                regroup(t + 2)
+            if in_range(t - 1, batches):
+                norms(t - 1)
+            if in_range(t - 1, feature_batches):
+                token_weights(t - 1)
+            for half in range(BANKS):
+                first, second = half * BANK_TILES, half * BANK_TILES + 1
+                if in_range(t, batches):
+                    multiply(t, first)
+                if half < FOLDED and in_range(t - 2, feature_batches):
+                    fold(t - 2, half)
+                if in_range(t, batches):
+                    multiply(t, second)
+                if half == 0 and in_range(t + 1, batches):
+                    quantise(t + 1, codes_pool)
+                if half == 1 and t - 1 == aspect_batch:
+                    store_q(t - 1)
+                if in_range(summed, feature_batches):
+                    group, part = divmod(summed, GROUP_BATCHES)
+                    reduce_tokens(group, part * BATCH_SLICES + half)
+            if in_range(summed, feature_batches) and summed % BLOCK_BATCHES == BLOCK_BATCHES - 1:
+                collect_block(summed // BLOCK_BATCHES)

@@ -18,24 +18,15 @@ D_IN = 512
 D_OUT = 512
 TOKENS = 32
 TILES = 4
-FOLDED = 2
-KEPT = TILES - FOLDED
-assert FOLDED <= KEPT
 BATCH_ROWS = TILES * P
-GROUP_BATCHES = 2
-GROUP_TILES = GROUP_BATCHES * TILES
-GROUP_ROWS = GROUP_TILES * P
-GROUP_SEGMENTS = GROUP_ROWS // TOKENS
-SEGMENT_PARTITIONS = TOKENS // GROUP_TILES
-BLOCK_GROUPS = P // GROUP_SEGMENTS
-BLOCK_BATCHES = BLOCK_GROUPS * GROUP_BATCHES
+BLOCK_BATCHES = TOKENS // TILES
 OUT_SLICES = D_OUT // P
-BATCH_SLICES = OUT_SLICES // GROUP_BATCHES
 WORDS = D_IN // 2
 BANK_TILES = 2
 BANKS = TILES // BANK_TILES
 ROW_BUFFERS = 4
-SUM_LAG = 4
+VECTOR_TILES = 2
+SUM_LAG = 2
 TINY = 1e-24
 
 FLOPS = 2 * (512 * 32 + 512) * D_IN * D_OUT
@@ -43,8 +34,7 @@ FLOPS = 2 * (512 * 32 + 512) * D_IN * D_OUT
 
 def tile_linearattention_pa_t_kernel(tc, feature, aspect_v, W, b, out_0, out_1):
     nc = tc.nc
-    tokens = feature.flatten_outer_dims()
-    feature_batches = tokens.shape[0] // BATCH_ROWS
+    feature_batches = feature.shape[0] * TOKENS // BATCH_ROWS
     aspect_batch = feature_batches
     batches = feature_batches + 1
 
@@ -54,8 +44,7 @@ def tile_linearattention_pa_t_kernel(tc, feature, aspect_v, W, b, out_0, out_1):
         rows_pool = ctx.enter_context(tc.tile_pool(name="rows", bufs=ROW_BUFFERS))
         grouped_pool = ctx.enter_context(tc.tile_pool(name="grouped", bufs=2))
         codes_pool = ctx.enter_context(tc.tile_pool(name="codes", bufs=2))
-        y_pool = ctx.enter_context(tc.tile_pool(name="y", bufs=(SUM_LAG + GROUP_BATCHES + 1) * TILES))
-        weights_pool = ctx.enter_context(tc.tile_pool(name="weights", bufs=SUM_LAG + GROUP_BATCHES + 1))
+        y_pool = ctx.enter_context(tc.tile_pool(name="y", bufs=(SUM_LAG + 2) * TILES))
         squares_pool = ctx.enter_context(tc.tile_pool(name="squares", bufs=TILES))
         norm_pool = ctx.enter_context(tc.tile_pool(name="norm", bufs=3))
         fm_pool = ctx.enter_context(tc.tile_pool(name="fm", bufs=2))
@@ -71,10 +60,7 @@ def tile_linearattention_pa_t_kernel(tc, feature, aspect_v, W, b, out_0, out_1):
         scales_of = {}
         y_of = {}
         sumsq_of = {}
-        floored_of = {}
         inverse_of = {}
-        weights_of = {}
-        ratio_of = {}
         fm_t_of = {}
         fm_t_sbuf_of = {}
 
@@ -87,35 +73,31 @@ def tile_linearattention_pa_t_kernel(tc, feature, aspect_v, W, b, out_0, out_1):
             if n == aspect_batch:
                 load(n, aspect_v.rearrange("(p j) k -> p j k", j=TILES))
             else:
-                group, part = divmod(n, GROUP_BATCHES)
-                group_rows = tokens[group * GROUP_ROWS : (group + 1) * GROUP_ROWS, :]
-                by_partition = group_rows.rearrange("(p j) k -> p j k", j=GROUP_TILES)
-                load(n, by_partition[:, part * TILES : (part + 1) * TILES, :])
+                block, part = divmod(n, BLOCK_BATCHES)
+                load(n, feature[block * P : (block + 1) * P, part * TILES : (part + 1) * TILES, :])
 
-        def transpose(n):
+        def transpose(n, h):
             words = rows_of[n][:].bitcast(F32)
-            blocks = BANK_TILES * WORDS // P
-            banks_of[n] = []
-            for h in range(BANKS):
-                bank = words_psum.tile([P, BANK_TILES * WORDS], F32, name="bank")
-                for block in range(blocks):
-                    j, u = divmod(h * blocks + block, 2)
-                    nc.tensor.transpose(
-                        out=bank[:, block * P : (block + 1) * P],
-                        in_=words[:, j * WORDS + u : (j + 1) * WORDS : 2],
-                        identity=identity[:],
-                    )
-                banks_of[n].append(bank)
-
-        def regroup(n):
-            grouped = grouped_pool.tile([P, TILES * P * 4], BF16, name="grouped", align_bytes=64)
-            pairs = grouped[:].bitcast(F32).rearrange("p (h j r u) -> p h j r u", h=BANKS, j=BANK_TILES, u=2)
-            for h in range(BANKS):
-                nc.scalar.copy(
-                    out=pairs[:, h],
-                    in_=banks_of[n][h][:].rearrange("p (j u r) -> p j r u", j=BANK_TILES, u=2),
+            bank = words_psum.tile([P, BANK_TILES * WORDS], F32, name="bank")
+            for block in range(BANK_TILES * WORDS // P):
+                j, u = divmod(block, 2)
+                start = (h * BANK_TILES + j) * WORDS
+                nc.tensor.transpose(
+                    out=bank[:, block * P : (block + 1) * P],
+                    in_=words[:, start + u : start + WORDS : 2],
+                    identity=identity[:],
                 )
-            grouped_of[n] = grouped
+            banks_of[n, h] = bank
+
+        def regroup(n, h):
+            if h == 0:
+                grouped = grouped_pool.tile([P, TILES * P * 4], BF16, name="grouped", align_bytes=64)
+                grouped_of[n] = grouped
+            pairs = grouped_of[n][:].bitcast(F32).rearrange("p (h j r u) -> p h j r u", h=BANKS, j=BANK_TILES, u=2)
+            nc.scalar.copy(
+                out=pairs[:, h],
+                in_=banks_of[n, h][:].rearrange("p (j u r) -> p j r u", j=BANK_TILES, u=2),
+            )
 
         def quantise(n, pool):
             codes = pool.tile([P, TILES * P], U32, name="codes", align_bytes=64)
@@ -150,46 +132,35 @@ def tile_linearattention_pa_t_kernel(tc, feature, aspect_v, W, b, out_0, out_1):
             inverse = norm_pool.tile([P, TILES], F32, name="inverse")
             nc.gpsimd.tensor_scalar_max(out=floored[:], in0=sumsq_of[n][:], scalar1=TINY)
             nc.gpsimd.tensor_tensor(out=inverse[:], in0=floored[:], in1=minus_half[:], op=POW)
-            floored_of[n] = floored
             inverse_of[n] = inverse
 
-        def token_weights(n):
-            inverse = inverse_of[n]
-            norm = norm_pool.tile([P, FOLDED], F32, name="norm")
-            ratio = norm_pool.tile([P, FOLDED], F32, name="ratio")
-            weights = weights_pool.tile([P, KEPT, GROUP_SEGMENTS], F32, name="weights")
-            nc.gpsimd.tensor_tensor(out=norm[:], in0=floored_of[n][:, :FOLDED], in1=inverse[:, :FOLDED], op=MULT)
-            nc.gpsimd.tensor_tensor(out=ratio[:], in0=norm[:], in1=inverse[:, KEPT:], op=MULT)
-            nc.gpsimd.tensor_tensor(
-                out=weights[:],
-                in0=membership[:].unsqueeze(1).to_broadcast([P, KEPT, GROUP_SEGMENTS]),
-                in1=inverse[:, :KEPT].unsqueeze(2).to_broadcast([P, KEPT, GROUP_SEGMENTS]),
-                op=MULT,
-            )
-            weights_of[n] = weights
-            ratio_of[n] = ratio
-
-        def fold(n, i):
-            kept = y_of[n, i]
-            nc.vector.scalar_tensor_tensor(
-                out=kept[:], in0=y_of[n, KEPT + i][:], scalar=ratio_of[n][:, i : i + 1], in1=kept[:], op0=MULT, op1=ADD
+        def normalise(n, j):
+            y = y_of[n, j]
+            engine = nc.gpsimd if j < TILES - VECTOR_TILES else nc.vector
+            engine.tensor_scalar(
+                out=y[:],
+                in0=y[:],
+                scalar1=inverse_of[n][:, j : j + 1],
+                scalar2=1.0 / TOKENS,
+                op0=MULT,
+                op1=MULT,
             )
 
-        def reduce_tokens(group, s):
-            block, place = divmod(group, BLOCK_GROUPS)
-            if place == 0 and s == 0:
+        def reduce_tokens(n, j):
+            block, part = divmod(n, BLOCK_BATCHES)
+            tile = part * TILES + j
+            if tile == 0:
                 fm_t = fm_t_psum.tile([P, OUT_SLICES * P], F32, name="fm_t")
                 fm_t_of[block] = fm_t
-            first = s * P + place * GROUP_SEGMENTS
-            for tile in range(GROUP_BATCHES * KEPT):
-                part, j = divmod(tile, KEPT)
-                n = group * GROUP_BATCHES + part
+            for s in range(OUT_SLICES):
+                cols = slice(s * P, (s + 1) * P)
                 nc.tensor.matmul(
-                    out=fm_t_of[block][:, first : first + GROUP_SEGMENTS],
-                    lhsT=y_of[n, j][:, s * P : (s + 1) * P],
-                    rhs=weights_of[n][:, j, :],
-                    start=(tile == 0),
-                    stop=(tile == GROUP_BATCHES * KEPT - 1),
+                    out=fm_t_of[block][:, cols],
+                    lhsT=y_of[n, j][:, cols],
+                    rhs=identity[:],
+                    is_transpose=True,
+                    start=(tile == 0 and s == 0),
+                    stop=(tile == TOKENS - 1 and s == OUT_SLICES - 1),
                 )
 
         def collect_block(block):
@@ -223,49 +194,39 @@ def tile_linearattention_pa_t_kernel(tc, feature, aspect_v, W, b, out_0, out_1):
         make_identity(nc, identity[:])
         minus_half = const.tile([P, TILES], F32, name="minus_half")
         nc.vector.memset(minus_half[:], -0.5)
-        membership = const.tile([P, GROUP_SEGMENTS], F32, name="membership")
-        nc.vector.tensor_reduce(
-            out=membership[:],
-            in_=identity[:].rearrange("p (c i) -> p c i", i=SEGMENT_PARTITIONS),
-            axis=mybir.AxisListType.X,
-            op=ADD,
-        )
-        nc.vector.tensor_scalar_mul(out=membership[:], in0=membership[:], scalar1=1.0 / TOKENS)
 
-        transpose("W")
-        regroup("W")
+        for h in range(BANKS):
+            transpose("W", h)
+            regroup("W", h)
         quantise("W", const)
 
         def in_range(n, end):
             return 0 <= n < end
 
-        for t in range(-2, batches + SUM_LAG):
+        for t in range(-2, batches + SUM_LAG + 1):
             summed, stored = t - SUM_LAG, t - SUM_LAG - 1
             if in_range(t + ROW_BUFFERS + 1, batches):
                 load_batch(t + ROW_BUFFERS + 1)
-            if in_range(stored, feature_batches) and stored % BLOCK_BATCHES == BLOCK_BATCHES - 1:
-                store_block(stored // BLOCK_BATCHES)
-            if in_range(t + 2, batches):
-                transpose(t + 2)
-                regroup(t + 2)
             if in_range(t - 1, batches):
                 norms(t - 1)
-            if in_range(t - 1, feature_batches):
-                token_weights(t - 1)
             for half in range(BANKS):
-                first, second = half * BANK_TILES, half * BANK_TILES + 1
-                if in_range(t, batches):
-                    multiply(t, first)
-                if half < FOLDED and in_range(t - 2, feature_batches):
-                    fold(t - 2, half)
-                if in_range(t, batches):
-                    multiply(t, second)
+                if in_range(t + 2, batches):
+                    transpose(t + 2, half)
+                    regroup(t + 2, half)
+                for j in range(half * BANK_TILES, (half + 1) * BANK_TILES):
+                    if in_range(summed, feature_batches):
+                        reduce_tokens(summed, j)
+                if half == 1 and in_range(stored, feature_batches) and stored % BLOCK_BATCHES == BLOCK_BATCHES - 1:
+                    store_block(stored // BLOCK_BATCHES)
+                for j in range(half * BANK_TILES, (half + 1) * BANK_TILES):
+                    if in_range(t, batches):
+                        multiply(t, j)
                 if half == 0 and in_range(t + 1, batches):
                     quantise(t + 1, codes_pool)
                 if half == 1 and t - 1 == aspect_batch:
                     store_q(t - 1)
-                if in_range(summed, feature_batches):
-                    group, part = divmod(summed, GROUP_BATCHES)
-                    reduce_tokens(group, part * BATCH_SLICES + half)
+            if in_range(t - 1, feature_batches):
+                for j in range(TILES):
+                    normalise(t - 1, j)
             if in_range(summed, feature_batches) and summed % BLOCK_BATCHES == BLOCK_BATCHES - 1:
                 collect_block(summed // BLOCK_BATCHES)

@@ -10,6 +10,7 @@ U8 = mybir.dt.uint8
 FP8X4 = mybir.dt.float8_e4m3fn_x4
 ADD = mybir.AluOpType.add
 MULT = mybir.AluOpType.mult
+MAX = mybir.AluOpType.max
 POW = mybir.AluOpType.pow
 SQUARE = mybir.ActivationFunctionType.Square
 
@@ -24,9 +25,12 @@ OUT_SLICES = D_OUT // P
 WORDS = D_IN // 2
 BANK_TILES = 2
 BANKS = TILES // BANK_TILES
+PLAIN_SLICE = OUT_SLICES - 1
 ROW_BUFFERS = 4
-VECTOR_TILES = 2
-SUM_LAG = 2
+FOLDED = 2
+KEPT = TILES - FOLDED
+BLOCK_SUMS = KEPT * BLOCK_BATCHES
+SUM_LAG = 3
 TINY = 1e-24
 
 FLOPS = 2 * (512 * 32 + 512) * D_IN * D_OUT
@@ -60,7 +64,7 @@ def tile_linearattention_pa_t_kernel(tc, feature, aspect_v, W, b, out_0, out_1):
         scales_of = {}
         y_of = {}
         sumsq_of = {}
-        inverse_of = {}
+        share_of = {}
         fm_t_of = {}
         fm_t_sbuf_of = {}
 
@@ -129,26 +133,33 @@ def tile_linearattention_pa_t_kernel(tc, feature, aspect_v, W, b, out_0, out_1):
 
         def norms(n):
             floored = norm_pool.tile([P, TILES], F32, name="floored")
-            inverse = norm_pool.tile([P, TILES], F32, name="inverse")
-            nc.gpsimd.tensor_scalar_max(out=floored[:], in0=sumsq_of[n][:], scalar1=TINY)
-            nc.gpsimd.tensor_tensor(out=inverse[:], in0=floored[:], in1=minus_half[:], op=POW)
-            inverse_of[n] = inverse
+            share = norm_pool.tile([P, TILES], F32, name="share")
+            nc.gpsimd.tensor_scalar(
+                out=floored[:], in0=sumsq_of[n][:], scalar1=TINY, scalar2=float(TOKENS**2), op0=MAX, op1=MULT
+            )
+            nc.gpsimd.tensor_tensor(out=share[:], in0=floored[:], in1=minus_half[:], op=POW)
+            share_of[n] = share
 
         def normalise(n, j):
             y = y_of[n, j]
-            engine = nc.gpsimd if j < TILES - VECTOR_TILES else nc.vector
-            engine.tensor_scalar(
-                out=y[:],
-                in0=y[:],
-                scalar1=inverse_of[n][:, j : j + 1],
-                scalar2=1.0 / TOKENS,
+            nc.gpsimd.tensor_scalar(
+                out=y[:], in0=y[:], scalar1=share_of[n][:, j : j + 1], scalar2=0.0, op0=MULT, op1=ADD
+            )
+
+        def fold(n, i):
+            kept = y_of[n, i]
+            nc.vector.scalar_tensor_tensor(
+                out=kept[:],
+                in0=y_of[n, KEPT + i][:],
+                scalar=share_of[n][:, KEPT + i : KEPT + i + 1],
+                in1=kept[:],
                 op0=MULT,
-                op1=MULT,
+                op1=ADD,
             )
 
         def reduce_tokens(n, j):
             block, part = divmod(n, BLOCK_BATCHES)
-            tile = part * TILES + j
+            tile = part * KEPT + j
             if tile == 0:
                 fm_t = fm_t_psum.tile([P, OUT_SLICES * P], F32, name="fm_t")
                 fm_t_of[block] = fm_t
@@ -158,9 +169,9 @@ def tile_linearattention_pa_t_kernel(tc, feature, aspect_v, W, b, out_0, out_1):
                     out=fm_t_of[block][:, cols],
                     lhsT=y_of[n, j][:, cols],
                     rhs=identity[:],
-                    is_transpose=True,
+                    is_transpose=(s != PLAIN_SLICE),
                     start=(tile == 0 and s == 0),
-                    stop=(tile == TOKENS - 1 and s == OUT_SLICES - 1),
+                    stop=(tile == BLOCK_SUMS - 1 and s == OUT_SLICES - 1),
                 )
 
         def collect_block(block):
@@ -178,11 +189,17 @@ def tile_linearattention_pa_t_kernel(tc, feature, aspect_v, W, b, out_0, out_1):
             nc.sync.dma_start(out=out_1[block * P : (block + 1) * P, :], in_=fm[:])
 
         def store_q(n):
-            inverse = inverse_of[n]
             q_rows = out_0.rearrange("(p j) m -> p j m", j=TILES)
             for j in range(TILES):
                 y = y_of[n, j]
-                nc.vector.tensor_scalar_mul(out=y[:], in0=y[:], scalar1=inverse[:, j : j + 1])
+                nc.vector.tensor_scalar(
+                    out=y[:],
+                    in0=y[:],
+                    scalar1=share_of[n][:, j : j + 1],
+                    scalar2=float(TOKENS),
+                    op0=MULT,
+                    op1=MULT,
+                )
                 nc.sync.dma_start(out=q_rows[:, j, :], in_=y[:])
 
         load("W", W.rearrange("(j p) k -> p j k", p=P))
@@ -209,24 +226,27 @@ def tile_linearattention_pa_t_kernel(tc, feature, aspect_v, W, b, out_0, out_1):
                 load_batch(t + ROW_BUFFERS + 1)
             if in_range(t - 1, batches):
                 norms(t - 1)
+            if in_range(t - 1, feature_batches):
+                for j in range(KEPT):
+                    normalise(t - 1, j)
             for half in range(BANKS):
                 if in_range(t + 2, batches):
                     transpose(t + 2, half)
                     regroup(t + 2, half)
-                for j in range(half * BANK_TILES, (half + 1) * BANK_TILES):
-                    if in_range(summed, feature_batches):
-                        reduce_tokens(summed, j)
                 if half == 1 and in_range(stored, feature_batches) and stored % BLOCK_BATCHES == BLOCK_BATCHES - 1:
                     store_block(stored // BLOCK_BATCHES)
+                if in_range(summed, feature_batches):
+                    for j in range(half, KEPT, BANKS):
+                        reduce_tokens(summed, j)
                 for j in range(half * BANK_TILES, (half + 1) * BANK_TILES):
                     if in_range(t, batches):
                         multiply(t, j)
                 if half == 0 and in_range(t + 1, batches):
                     quantise(t + 1, codes_pool)
+                if in_range(t - 2, feature_batches):
+                    for i in range(half, FOLDED, BANKS):
+                        fold(t - 2, i)
                 if half == 1 and t - 1 == aspect_batch:
                     store_q(t - 1)
-            if in_range(t - 1, feature_batches):
-                for j in range(TILES):
-                    normalise(t - 1, j)
             if in_range(summed, feature_batches) and summed % BLOCK_BATCHES == BLOCK_BATCHES - 1:
                 collect_block(summed // BLOCK_BATCHES)

@@ -142,9 +142,7 @@ def tile_linearattention_pa_t_kernel(tc, feature, aspect_v, W, b, out_0, out_1):
 
         def normalise(n, j):
             y = y_of[n, j]
-            nc.gpsimd.tensor_scalar(
-                out=y[:], in0=y[:], scalar1=share_of[n][:, j : j + 1], scalar2=0.0, op0=MULT, op1=ADD
-            )
+            nc.vector.tensor_scalar_mul(out=y[:], in0=y[:], scalar1=share_of[n][:, j : j + 1])
 
         def fold(n, i):
             kept = y_of[n, i]
@@ -226,9 +224,6 @@ def tile_linearattention_pa_t_kernel(tc, feature, aspect_v, W, b, out_0, out_1):
                 load_batch(t + ROW_BUFFERS + 1)
             if in_range(t - 1, batches):
                 norms(t - 1)
-            if in_range(t - 1, feature_batches):
-                for j in range(KEPT):
-                    normalise(t - 1, j)
             for half in range(BANKS):
                 if in_range(t + 2, batches):
                     transpose(t + 2, half)
@@ -246,6 +241,9 @@ def tile_linearattention_pa_t_kernel(tc, feature, aspect_v, W, b, out_0, out_1):
                 if in_range(t - 2, feature_batches):
                     for i in range(half, FOLDED, BANKS):
                         fold(t - 2, i)
+                if half == 1 and in_range(t - 1, feature_batches):
+                    for j in range(KEPT):
+                        normalise(t - 1, j)
                 if half == 1 and t - 1 == aspect_batch:
                     store_q(t - 1)
             if in_range(summed, feature_batches) and summed % BLOCK_BATCHES == BLOCK_BATCHES - 1:

@@ -12,6 +12,7 @@ ADD = mybir.AluOpType.add
 MULT = mybir.AluOpType.mult
 MAX = mybir.AluOpType.max
 POW = mybir.AluOpType.pow
+COPY = mybir.ActivationFunctionType.Copy
 SQUARE = mybir.ActivationFunctionType.Square
 
 P = 128
@@ -25,11 +26,13 @@ OUT_SLICES = D_OUT // P
 WORDS = D_IN // 2
 BANK_TILES = 2
 BANKS = TILES // BANK_TILES
-PLAIN_SLICE = OUT_SLICES - 1
 ROW_BUFFERS = 4
-FOLDED = 2
+FOLDED = 1
+SCALAR_TILES = 1
 KEPT = TILES - FOLDED
 BLOCK_SUMS = KEPT * BLOCK_BATCHES
+UNITS = KEPT * OUT_SLICES
+PLAIN_UNITS = 1
 SUM_LAG = 3
 TINY = 1e-24
 
@@ -54,8 +57,7 @@ def tile_linearattention_pa_t_kernel(tc, feature, aspect_v, W, b, out_0, out_1):
         fm_pool = ctx.enter_context(tc.tile_pool(name="fm", bufs=2))
         words_psum = ctx.enter_context(tc.psum_pool(name="words_psum", bufs=BANKS))
         product_psum = ctx.enter_context(tc.psum_pool(name="product_psum", bufs=TILES))
-        fm_t_psum = ctx.enter_context(tc.psum_pool(name="fm_t_psum", bufs=1))
-        fm_psum = ctx.enter_context(tc.psum_pool(name="fm_psum", bufs=1))
+        fm_t_psum = ctx.enter_context(tc.psum_pool(name="fm_t_psum", bufs=2))
 
         rows_of = {}
         banks_of = {}
@@ -142,7 +144,11 @@ def tile_linearattention_pa_t_kernel(tc, feature, aspect_v, W, b, out_0, out_1):
 
         def normalise(n, j):
             y = y_of[n, j]
-            nc.vector.tensor_scalar_mul(out=y[:], in0=y[:], scalar1=share_of[n][:, j : j + 1])
+            share = share_of[n][:, j : j + 1]
+            if j < KEPT - SCALAR_TILES:
+                nc.vector.tensor_scalar_mul(out=y[:], in0=y[:], scalar1=share)
+            else:
+                nc.scalar.activation(out=y[:], in_=y[:], func=COPY, scale=share)
 
         def fold(n, i):
             kept = y_of[n, i]
@@ -155,22 +161,22 @@ def tile_linearattention_pa_t_kernel(tc, feature, aspect_v, W, b, out_0, out_1):
                 op1=ADD,
             )
 
-        def reduce_tokens(n, j):
+        def reduce_tokens(n, unit):
+            j, s = divmod(unit, OUT_SLICES)
             block, part = divmod(n, BLOCK_BATCHES)
             tile = part * KEPT + j
-            if tile == 0:
+            if tile == 0 and s == 0:
                 fm_t = fm_t_psum.tile([P, OUT_SLICES * P], F32, name="fm_t")
                 fm_t_of[block] = fm_t
-            for s in range(OUT_SLICES):
-                cols = slice(s * P, (s + 1) * P)
-                nc.tensor.matmul(
-                    out=fm_t_of[block][:, cols],
-                    lhsT=y_of[n, j][:, cols],
-                    rhs=identity[:],
-                    is_transpose=(s != PLAIN_SLICE),
-                    start=(tile == 0 and s == 0),
-                    stop=(tile == BLOCK_SUMS - 1 and s == OUT_SLICES - 1),
-                )
+            cols = slice(s * P, (s + 1) * P)
+            nc.tensor.matmul(
+                out=fm_t_of[block][:, cols],
+                lhsT=y_of[n, j][:, cols],
+                rhs=identity[:],
+                is_transpose=(unit < UNITS - PLAIN_UNITS),
+                start=(tile == 0 and s == 0),
+                stop=(tile == BLOCK_SUMS - 1 and s == OUT_SLICES - 1),
+            )
 
         def collect_block(block):
             fm_t_sbuf = fm_pool.tile([P, OUT_SLICES * P], F32, name="fm_t_sbuf")
@@ -178,7 +184,7 @@ def tile_linearattention_pa_t_kernel(tc, feature, aspect_v, W, b, out_0, out_1):
             fm_t_sbuf_of[block] = fm_t_sbuf
 
         def store_block(block):
-            fm_bank = fm_psum.tile([P, D_OUT], F32, name="fm_bank")
+            fm_bank = product_psum.tile([P, D_OUT], F32, name="product")
             for s in range(OUT_SLICES):
                 cols = slice(s * P, (s + 1) * P)
                 nc.tensor.transpose(out=fm_bank[:, cols], in_=fm_t_sbuf_of[block][:, cols], identity=identity[:])
@@ -231,18 +237,21 @@ def tile_linearattention_pa_t_kernel(tc, feature, aspect_v, W, b, out_0, out_1):
                 if half == 1 and in_range(stored, feature_batches) and stored % BLOCK_BATCHES == BLOCK_BATCHES - 1:
                     store_block(stored // BLOCK_BATCHES)
                 if in_range(summed, feature_batches):
-                    for j in range(half, KEPT, BANKS):
-                        reduce_tokens(summed, j)
+                    for unit in range(half * UNITS // BANKS, (half + 1) * UNITS // BANKS):
+                        reduce_tokens(summed, unit)
                 for j in range(half * BANK_TILES, (half + 1) * BANK_TILES):
                     if in_range(t, batches):
                         multiply(t, j)
+                if half == 0 and in_range(t - 1, feature_batches):
+                    for j in range(KEPT - SCALAR_TILES, KEPT):
+                        normalise(t - 1, j)
                 if half == 0 and in_range(t + 1, batches):
                     quantise(t + 1, codes_pool)
-                if in_range(t - 2, feature_batches):
-                    for i in range(half, FOLDED, BANKS):
+                if half == 0 and in_range(t - 2, feature_batches):
+                    for i in range(FOLDED):
                         fold(t - 2, i)
                 if half == 1 and in_range(t - 1, feature_batches):
-                    for j in range(KEPT):
+                    for j in range(KEPT - SCALAR_TILES):
                         normalise(t - 1, j)
                 if half == 1 and t - 1 == aspect_batch:
                     store_q(t - 1)

@@ -32,7 +32,7 @@ SCALAR_TILES = 1
 KEPT = TILES - FOLDED
 BLOCK_SUMS = KEPT * BLOCK_BATCHES
 UNITS = KEPT * OUT_SLICES
-PLAIN_UNITS = 1
+RUN_UNITS = UNITS // BANKS
 SUM_LAG = 3
 TINY = 1e-24
 
@@ -173,7 +173,7 @@ def tile_linearattention_pa_t_kernel(tc, feature, aspect_v, W, b, out_0, out_1):
                 out=fm_t_of[block][:, cols],
                 lhsT=y_of[n, j][:, cols],
                 rhs=identity[:],
-                is_transpose=(unit < UNITS - PLAIN_UNITS),
+                is_transpose=((unit + 1) % RUN_UNITS != 0),
                 start=(tile == 0 and s == 0),
                 stop=(tile == BLOCK_SUMS - 1 and s == OUT_SLICES - 1),
             )
@@ -237,7 +237,7 @@ def tile_linearattention_pa_t_kernel(tc, feature, aspect_v, W, b, out_0, out_1):
                 if half == 1 and in_range(stored, feature_batches) and stored % BLOCK_BATCHES == BLOCK_BATCHES - 1:
                     store_block(stored // BLOCK_BATCHES)
                 if in_range(summed, feature_batches):
-                    for unit in range(half * UNITS // BANKS, (half + 1) * UNITS // BANKS):
+                    for unit in range(half * RUN_UNITS, (half + 1) * RUN_UNITS):
                         reduce_tokens(summed, unit)
                 for j in range(half * BANK_TILES, (half + 1) * BANK_TILES):
                     if in_range(t, batches):

@@ -33,7 +33,7 @@ KEPT = TILES - FOLDED
 BLOCK_SUMS = KEPT * BLOCK_BATCHES
 UNITS = KEPT * OUT_SLICES
 RUN_UNITS = UNITS // BANKS
-SUM_LAG = 3
+SUM_LAG = 4
 TINY = 1e-24
 
 FLOPS = 2 * (512 * 32 + 512) * D_IN * D_OUT
@@ -242,9 +242,9 @@ def tile_linearattention_pa_t_kernel(tc, feature, aspect_v, W, b, out_0, out_1):
                 for j in range(half * BANK_TILES, (half + 1) * BANK_TILES):
                     if in_range(t, batches):
                         multiply(t, j)
-                if half == 0 and in_range(t - 1, feature_batches):
+                if half == 0 and in_range(t - 2, feature_batches):
                     for j in range(KEPT - SCALAR_TILES, KEPT):
-                        normalise(t - 1, j)
+                        normalise(t - 2, j)
                 if half == 0 and in_range(t + 1, batches):
                     quantise(t + 1, codes_pool)
                 if half == 0 and in_range(t - 2, feature_batches):

@@ -28,7 +28,7 @@ BANK_TILES = 2
 BANKS = TILES // BANK_TILES
 ROW_BUFFERS = 4
 FOLDED = 1
-SCALAR_TILES = 1
+SCALAR_TILES = (0, 1)
 KEPT = TILES - FOLDED
 BLOCK_SUMS = KEPT * BLOCK_BATCHES
 UNITS = KEPT * OUT_SLICES
@@ -84,7 +84,10 @@ def tile_linearattention_pa_t_kernel(tc, feature, aspect_v, W, b, out_0, out_1):
 
         def transpose(n, h):
             words = rows_of[n][:].bitcast(F32)
-            bank = words_psum.tile([P, BANK_TILES * WORDS], F32, name="bank")
+            if n == "W":
+                bank = product_psum.tile([P, BANK_TILES * WORDS], F32, name="product")
+            else:
+                bank = words_psum.tile([P, BANK_TILES * WORDS], F32, name="bank")
             for block in range(BANK_TILES * WORDS // P):
                 j, u = divmod(block, 2)
                 start = (h * BANK_TILES + j) * WORDS
@@ -100,7 +103,8 @@ def tile_linearattention_pa_t_kernel(tc, feature, aspect_v, W, b, out_0, out_1):
                 grouped = grouped_pool.tile([P, TILES * P * 4], BF16, name="grouped", align_bytes=64)
                 grouped_of[n] = grouped
             pairs = grouped_of[n][:].bitcast(F32).rearrange("p (h j r u) -> p h j r u", h=BANKS, j=BANK_TILES, u=2)
-            nc.scalar.copy(
+            copy = nc.vector.tensor_copy if n == "W" else nc.scalar.copy
+            copy(
                 out=pairs[:, h],
                 in_=banks_of[n, h][:].rearrange("p (j u r) -> p j r u", j=BANK_TILES, u=2),
             )
@@ -145,7 +149,7 @@ def tile_linearattention_pa_t_kernel(tc, feature, aspect_v, W, b, out_0, out_1):
         def normalise(n, j):
             y = y_of[n, j]
             share = share_of[n][:, j : j + 1]
-            if j < KEPT - SCALAR_TILES:
+            if j < KEPT - SCALAR_TILES[n % 2]:
                 nc.vector.tensor_scalar_mul(out=y[:], in0=y[:], scalar1=share)
             else:
                 nc.scalar.activation(out=y[:], in_=y[:], func=COPY, scale=share)
@@ -243,7 +247,7 @@ def tile_linearattention_pa_t_kernel(tc, feature, aspect_v, W, b, out_0, out_1):
                     if in_range(t, batches):
                         multiply(t, j)
                 if half == 0 and in_range(t - 2, feature_batches):
-                    for j in range(KEPT - SCALAR_TILES, KEPT):
+                    for j in range(KEPT - SCALAR_TILES[t % 2], KEPT):
                         normalise(t - 2, j)
                 if half == 0 and in_range(t + 1, batches):
                     quantise(t + 1, codes_pool)
@@ -251,7 +255,7 @@ def tile_linearattention_pa_t_kernel(tc, feature, aspect_v, W, b, out_0, out_1):
                     for i in range(FOLDED):
                         fold(t - 2, i)
                 if half == 1 and in_range(t - 1, feature_batches):
-                    for j in range(KEPT - SCALAR_TILES):
+                    for j in range(KEPT - SCALAR_TILES[(t - 1) % 2]):
                         normalise(t - 1, j)
                 if half == 1 and t - 1 == aspect_batch:
                     store_q(t - 1)

@@ -28,7 +28,7 @@ BANK_TILES = 2
 BANKS = TILES // BANK_TILES
 ROW_BUFFERS = 4
 FOLDED = 1
-SCALAR_TILES = (0, 1)
+VECTOR_TILE, GPSIMD_TILE, SCALAR_TILE = 0, 1, 2
 KEPT = TILES - FOLDED
 BLOCK_SUMS = KEPT * BLOCK_BATCHES
 UNITS = KEPT * OUT_SLICES
@@ -133,7 +133,7 @@ def tile_linearattention_pa_t_kernel(tc, feature, aspect_v, W, b, out_0, out_1):
             )
             y = y_pool.tile([P, D_OUT], F32, name="y")
             y_of[n, j] = y
-            nc.vector.tensor_tensor(out=y[:], in0=product[:], in1=bias[:], op=ADD)
+            nc.vector.tensor_tensor(out=y[:], in0=bias[:], in1=product[:], op=ADD)
             squares = squares_pool.tile([P, D_OUT], BF16, name="squares")
             nc.scalar.activation(out=squares[:], in_=y[:], func=SQUARE, accum_out=sumsq_of[n][:, j : j + 1])
 
@@ -149,8 +149,10 @@ def tile_linearattention_pa_t_kernel(tc, feature, aspect_v, W, b, out_0, out_1):
         def normalise(n, j):
             y = y_of[n, j]
             share = share_of[n][:, j : j + 1]
-            if j < KEPT - SCALAR_TILES[n % 2]:
+            if j == VECTOR_TILE:
                 nc.vector.tensor_scalar_mul(out=y[:], in0=y[:], scalar1=share)
+            elif j == GPSIMD_TILE:
+                nc.gpsimd.tensor_scalar(out=y[:], in0=y[:], scalar1=share, scalar2=0.0, op0=MULT, op1=ADD)
             else:
                 nc.scalar.activation(out=y[:], in_=y[:], func=COPY, scale=share)
 
@@ -232,6 +234,8 @@ def tile_linearattention_pa_t_kernel(tc, feature, aspect_v, W, b, out_0, out_1):
             summed, stored = t - SUM_LAG, t - SUM_LAG - 1
             if in_range(t + ROW_BUFFERS + 1, batches):
                 load_batch(t + ROW_BUFFERS + 1)
+            if in_range(t - 2, feature_batches):
+                normalise(t - 2, GPSIMD_TILE)
             if in_range(t - 1, batches):
                 norms(t - 1)
             for half in range(BANKS):
@@ -247,16 +251,14 @@ def tile_linearattention_pa_t_kernel(tc, feature, aspect_v, W, b, out_0, out_1):
                     if in_range(t, batches):
                         multiply(t, j)
                 if half == 0 and in_range(t - 2, feature_batches):
-                    for j in range(KEPT - SCALAR_TILES[t % 2], KEPT):
-                        normalise(t - 2, j)
+                    normalise(t - 2, SCALAR_TILE)
                 if half == 0 and in_range(t + 1, batches):
                     quantise(t + 1, codes_pool)
                 if half == 0 and in_range(t - 2, feature_batches):
                     for i in range(FOLDED):
                         fold(t - 2, i)
                 if half == 1 and in_range(t - 1, feature_batches):
-                    for j in range(KEPT - SCALAR_TILES[(t - 1) % 2]):
-                        normalise(t - 1, j)
+                    normalise(t - 1, VECTOR_TILE)
                 if half == 1 and t - 1 == aspect_batch:
                     store_q(t - 1)
             if in_range(summed, feature_batches) and summed % BLOCK_BATCHES == BLOCK_BATCHES - 1:

from contextlib import ExitStack

import concourse.mybir as mybir
from concourse.masks import make_identity

F32 = mybir.dt.float32
BF16 = mybir.dt.bfloat16
U32 = mybir.dt.uint32
U8 = mybir.dt.uint8
FP8X4 = mybir.dt.float8_e4m3fn_x4
ADD = mybir.AluOpType.add
MULT = mybir.AluOpType.mult
MAX = mybir.AluOpType.max
POW = mybir.AluOpType.pow
COPY = mybir.ActivationFunctionType.Copy
SQUARE = mybir.ActivationFunctionType.Square

P = 128
D_IN = 512
D_OUT = 512
TOKENS = 32
TILES = 4
BATCH_ROWS = TILES * P
BLOCK_BATCHES = TOKENS // TILES
OUT_SLICES = D_OUT // P
WORDS = D_IN // 2
BANK_TILES = 2
BANKS = TILES // BANK_TILES
ROW_BUFFERS = 4
FOLDED = 1
VECTOR_TILE, GPSIMD_TILE, SCALAR_TILE = 0, 1, 2
KEPT = TILES - FOLDED
BLOCK_SUMS = KEPT * BLOCK_BATCHES
UNITS = KEPT * OUT_SLICES
RUN_UNITS = UNITS // BANKS
SUM_LAG = 4
TINY = 1e-24

FLOPS = 2 * (512 * 32 + 512) * D_IN * D_OUT


def tile_linearattention_pa_t_kernel(tc, feature, aspect_v, W, b, out_0, out_1):
    nc = tc.nc
    feature_batches = feature.shape[0] * TOKENS // BATCH_ROWS
    aspect_batch = feature_batches
    batches = feature_batches + 1

    with ExitStack() as ctx:
        ctx.enter_context(tc.manual_schedule())
        const = ctx.enter_context(tc.tile_pool(name="const", bufs=1))
        rows_pool = ctx.enter_context(tc.tile_pool(name="rows", bufs=ROW_BUFFERS))
        grouped_pool = ctx.enter_context(tc.tile_pool(name="grouped", bufs=2))
        codes_pool = ctx.enter_context(tc.tile_pool(name="codes", bufs=2))
        y_pool = ctx.enter_context(tc.tile_pool(name="y", bufs=(SUM_LAG + 2) * TILES))
        squares_pool = ctx.enter_context(tc.tile_pool(name="squares", bufs=TILES))
        norm_pool = ctx.enter_context(tc.tile_pool(name="norm", bufs=3))
        fm_pool = ctx.enter_context(tc.tile_pool(name="fm", bufs=2))
        words_psum = ctx.enter_context(tc.psum_pool(name="words_psum", bufs=BANKS))
        product_psum = ctx.enter_context(tc.psum_pool(name="product_psum", bufs=TILES))
        fm_t_psum = ctx.enter_context(tc.psum_pool(name="fm_t_psum", bufs=2))

        rows_of = {}
        banks_of = {}
        grouped_of = {}
        codes_of = {}
        scales_of = {}
        y_of = {}
        sumsq_of = {}
        share_of = {}
        fm_t_of = {}
        fm_t_sbuf_of = {}

        def load(n, dram_view):
            rows = rows_pool.tile([P, TILES * D_IN], BF16, name="rows")
            nc.sync.dma_start(out=rows[:].rearrange("p (j k) -> p j k", j=TILES), in_=dram_view)
            rows_of[n] = rows

        def load_batch(n):
            if n == aspect_batch:
                load(n, aspect_v.rearrange("(p j) k -> p j k", j=TILES))
            else:
                block, part = divmod(n, BLOCK_BATCHES)
                load(n, feature[block * P : (block + 1) * P, part * TILES : (part + 1) * TILES, :])

        def transpose(n, h):
            words = rows_of[n][:].bitcast(F32)
            if n == "W":
                bank = product_psum.tile([P, BANK_TILES * WORDS], F32, name="product")
            else:
                bank = words_psum.tile([P, BANK_TILES * WORDS], F32, name="bank")
            for block in range(BANK_TILES * WORDS // P):
                j, u = divmod(block, 2)
                start = (h * BANK_TILES + j) * WORDS
                nc.tensor.transpose(
                    out=bank[:, block * P : (block + 1) * P],
                    in_=words[:, start + u : start + WORDS : 2],
                    identity=identity[:],
                )
            banks_of[n, h] = bank

        def regroup(n, h):
            if h == 0:
                grouped = grouped_pool.tile([P, TILES * P * 4], BF16, name="grouped", align_bytes=64)
                grouped_of[n] = grouped
            pairs = grouped_of[n][:].bitcast(F32).rearrange("p (h j r u) -> p h j r u", h=BANKS, j=BANK_TILES, u=2)
            copy = nc.vector.tensor_copy if n == "W" else nc.scalar.copy
            copy(
                out=pairs[:, h],
                in_=banks_of[n, h][:].rearrange("p (j u r) -> p j r u", j=BANK_TILES, u=2),
            )

        def quantise(n, pool):
            codes = pool.tile([P, TILES * P], U32, name="codes", align_bytes=64)
            scales = pool.tile([P, TILES * P], U8, name="scales", align_bytes=64)
            nc.vector.quantize_mx(out=codes[:].bitcast(FP8X4), scales=scales[:], in_=grouped_of[n][:])
            codes_of[n] = codes
            scales_of[n] = scales

        def multiply(n, j):
            if j == 0:
                sumsq = norm_pool.tile([P, TILES], F32, name="sumsq")
                sumsq_of[n] = sumsq
            cols = slice(j * P, (j + 1) * P)
            product = product_psum.tile([P, D_OUT], F32, name="product")
            nc.tensor.matmul_mx(
                out=product[:],
                lhsT=codes_of[n][:, cols].bitcast(FP8X4),
                lhsT_scale=scales_of[n][:, cols],
                rhs=codes_of["W"][:].bitcast(FP8X4),
                rhs_scale=scales_of["W"][:],
                start=True,
                stop=True,
            )
            y = y_pool.tile([P, D_OUT], F32, name="y")
            y_of[n, j] = y
            nc.vector.tensor_tensor(out=y[:], in0=bias[:], in1=product[:], op=ADD)
            squares = squares_pool.tile([P, D_OUT], BF16, name="squares")
            nc.scalar.activation(out=squares[:], in_=y[:], func=SQUARE, accum_out=sumsq_of[n][:, j : j + 1])

        def norms(n):
            floored = norm_pool.tile([P, TILES], F32, name="floored")
            share = norm_pool.tile([P, TILES], F32, name="share")
            nc.gpsimd.tensor_scalar(
                out=floored[:], in0=sumsq_of[n][:], scalar1=TINY, scalar2=float(TOKENS**2), op0=MAX, op1=MULT
            )
            nc.gpsimd.tensor_tensor(out=share[:], in0=floored[:], in1=minus_half[:], op=POW)
            share_of[n] = share

        def normalise(n, j):
            y = y_of[n, j]
            share = share_of[n][:, j : j + 1]
            if j == VECTOR_TILE:
                nc.vector.tensor_scalar_mul(out=y[:], in0=y[:], scalar1=share)
            elif j == GPSIMD_TILE:
                nc.gpsimd.tensor_scalar(out=y[:], in0=y[:], scalar1=share, scalar2=0.0, op0=MULT, op1=ADD)
            else:
                nc.scalar.activation(out=y[:], in_=y[:], func=COPY, scale=share)

        def fold(n, i):
            kept = y_of[n, i]
            nc.vector.scalar_tensor_tensor(
                out=kept[:],
                in0=y_of[n, KEPT + i][:],
                scalar=share_of[n][:, KEPT + i : KEPT + i + 1],
                in1=kept[:],
                op0=MULT,
                op1=ADD,
            )

        def reduce_tokens(n, unit):
            j, s = divmod(unit, OUT_SLICES)
            block, part = divmod(n, BLOCK_BATCHES)
            tile = part * KEPT + j
            if tile == 0 and s == 0:
                fm_t = fm_t_psum.tile([P, OUT_SLICES * P], F32, name="fm_t")
                fm_t_of[block] = fm_t
            cols = slice(s * P, (s + 1) * P)
            nc.tensor.matmul(
                out=fm_t_of[block][:, cols],
                lhsT=y_of[n, j][:, cols],
                rhs=identity[:],
                is_transpose=((unit + 1) % RUN_UNITS != 0),
                start=(tile == 0 and s == 0),
                stop=(tile == BLOCK_SUMS - 1 and s == OUT_SLICES - 1),
            )

        def collect_block(block):
            fm_t_sbuf = fm_pool.tile([P, OUT_SLICES * P], F32, name="fm_t_sbuf")
            nc.vector.tensor_copy(out=fm_t_sbuf[:], in_=fm_t_of[block][:])
            fm_t_sbuf_of[block] = fm_t_sbuf

        def store_block(block):
            fm_bank = product_psum.tile([P, D_OUT], F32, name="product")
            for s in range(OUT_SLICES):
                cols = slice(s * P, (s + 1) * P)
                nc.tensor.transpose(out=fm_bank[:, cols], in_=fm_t_sbuf_of[block][:, cols], identity=identity[:])
            fm = fm_pool.tile([P, D_OUT], F32, name="fm")
            nc.scalar.copy(out=fm[:], in_=fm_bank[:])
            nc.sync.dma_start(out=out_1[block * P : (block + 1) * P, :], in_=fm[:])

        def store_q(n):
            q_rows = out_0.rearrange("(p j) m -> p j m", j=TILES)
            for j in range(TILES):
                y = y_of[n, j]
                nc.vector.tensor_scalar(
                    out=y[:],
                    in0=y[:],
                    scalar1=share_of[n][:, j : j + 1],
                    scalar2=float(TOKENS),
                    op0=MULT,
                    op1=MULT,
                )
                nc.sync.dma_start(out=q_rows[:, j, :], in_=y[:])

        load("W", W.rearrange("(j p) k -> p j k", p=P))
        for n in range(ROW_BUFFERS - 1):
            load_batch(n)
        bias = const.tile([P, D_OUT], BF16, name="bias")
        nc.scalar.dma_start(out=bias[:], in_=b.partition_broadcast(P))
        identity = const.tile([P, P], F32, name="identity")
        make_identity(nc, identity[:])
        minus_half = const.tile([P, TILES], F32, name="minus_half")
        nc.vector.memset(minus_half[:], -0.5)

        for h in range(BANKS):
            transpose("W", h)
            regroup("W", h)
        quantise("W", const)

        def in_range(n, end):
            return 0 <= n < end

        for t in range(-2, batches + SUM_LAG + 1):
            summed, stored = t - SUM_LAG, t - SUM_LAG - 1
            if in_range(t + ROW_BUFFERS + 1, batches):
                load_batch(t + ROW_BUFFERS + 1)
            if in_range(t - 2, feature_batches):
                normalise(t - 2, GPSIMD_TILE)
            if in_range(t - 1, batches):
                norms(t - 1)
            for half in range(BANKS):
                if in_range(t + 2, batches):
                    transpose(t + 2, half)
                    regroup(t + 2, half)
                if half == 1 and in_range(stored, feature_batches) and stored % BLOCK_BATCHES == BLOCK_BATCHES - 1:
                    store_block(stored // BLOCK_BATCHES)
                if in_range(summed, feature_batches):
                    for unit in range(half * RUN_UNITS, (half + 1) * RUN_UNITS):
                        reduce_tokens(summed, unit)
                for j in range(half * BANK_TILES, (half + 1) * BANK_TILES):
                    if in_range(t, batches):
                        multiply(t, j)
                if half == 0 and in_range(t - 2, feature_batches):
                    normalise(t - 2, SCALAR_TILE)
                if half == 0 and in_range(t + 1, batches):
                    quantise(t + 1, codes_pool)
                if half == 0 and in_range(t - 2, feature_batches):
                    for i in range(FOLDED):
                        fold(t - 2, i)
                if half == 1 and in_range(t - 1, feature_batches):
                    normalise(t - 1, VECTOR_TILE)
                if half == 1 and t - 1 == aspect_batch:
                    store_q(t - 1)
            if in_range(summed, feature_batches) and summed % BLOCK_BATCHES == BLOCK_BATCHES - 1:
                collect_block(summed // BLOCK_BATCHES)
